import numpy as np
import ml_dtypes


BF16 = ml_dtypes.bfloat16


def bf(x):
    return np.asarray(x, np.float32).astype(BF16)


def f64(x):
    return np.asarray(x).astype(np.float64)


E2M1 = np.array([0.0, 0.5, 1.0, 1.5, 2.0, 3.0, 4.0, 6.0, -0.0, -0.5, -1.0, -1.5, -2.0, -3.0, -4.0, -6.0])


def pack_weight(w, fmt):
    k, n = w.shape
    w = f64(bf(w)).reshape(k // 32, 32, n)
    amax = np.abs(w).max(1)
    if fmt == "e4m3":
        byte = np.frexp(amax)[1] - 1 + 127 - 7
    else:
        mant, ex = np.frexp(amax / 6.0)
        byte = np.where(mant > 0.5, ex, ex - 1) + 127
    byte = np.clip(np.where(amax > 0, byte, 1), 1, 254)
    scaled = (w * np.exp2(127.0 - byte)[:, None, :]).reshape(k, n).astype(np.float32)
    by_word = np.ascontiguousarray(scaled.reshape(k // 512, 128, 4, n).transpose(0, 1, 3, 2))
    if fmt == "e4m3":
        words = by_word.astype(ml_dtypes.float8_e4m3fn).view(np.uint8)
    else:
        c = by_word.astype(ml_dtypes.float4_e2m1fn).view(np.uint8) & 0xF
        words = c[..., 0::2] | (c[..., 1::2] << 4)
    return np.ascontiguousarray(words), np.ascontiguousarray(byte.astype(np.uint8).reshape(k // 512, 16, n))


def unpack_weight(words, scales, fmt):
    g, p, n, _ = words.shape
    if fmt == "e4m3":
        vals = np.ascontiguousarray(words).view(ml_dtypes.float8_e4m3fn).astype(np.float64)
    else:
        nib = np.empty((g, p, n, 4), np.uint8)
        nib[..., 0::2] = words & 0xF
        nib[..., 1::2] = words >> 4
        vals = E2M1[nib]
    vals = vals * np.repeat(np.exp2(scales.astype(np.float64) - 127.0), 8, axis=1)[..., None]
    return vals.transpose(0, 1, 3, 2).reshape(g * 512, n)

def pack4(w):
    words, scales = pack_weight(w, "e2m1")
    return words.reshape(words.shape[0], 128, -1), scales


def unpack4(words, scales):
    return unpack_weight(words.reshape(words.shape[0], 128, -1, 2), scales, "e2m1")


def kspread(k):
    return np.exp2(np.repeat(np.random.randint(-6, 7, k // 32), 32).astype(np.float64))


B, IN, L = 512, 1024, 1536


def sigmoid(v):
    return 1.0 / (1.0 + np.exp(-v))


def setup_inputs():
    s = kspread(IN)
    inp = np.random.standard_normal((B, IN)) * s
    input_words, input_scales = pack4(inp.reshape(B, IN).T)
    h0 = bf(np.random.standard_normal((B, L)))
    gh0 = bf(np.random.standard_normal((B, 3 * L)) * 0.75)
    w = np.random.standard_normal((3 * L, IN)) * 0.7 / np.sqrt(IN) / s
    words, scales = pack4(w.T)
    b_ih0 = bf(np.random.standard_normal(3 * L) * 0.3)
    return {"input_words": input_words,
            "input_scales": input_scales,
            "h0": h0,
            "gh0": gh0,
            "W_ih0_words": words,
            "W_ih0_scales": scales,
            "b_ih0": b_ih0}


def reference(input_words, input_scales, h0, gh0, W_ih0_words, W_ih0_scales, b_ih0):
    h, gh = f64(h0), f64(gh0)
    gi = (unpack4(input_words, input_scales).T @ unpack4(W_ih0_words, W_ih0_scales)) + f64(b_ih0)
    i_r, i_z, i_n = gi[:, :L], gi[:, L:2 * L], gi[:, 2 * L:]
    h_r, h_z, h_n = gh[:, :L], gh[:, L:2 * L], gh[:, 2 * L:]
    r = sigmoid(i_r + h_r)
    z = sigmoid(i_z + h_z)
    n = np.tanh(i_n + r * h_n)
    return (1.0 - z) * n + z * h

from contextlib import ExitStack

import concourse.mybir as mybir
from concourse.masks import make_identity

F32 = mybir.dt.float32
BF16 = mybir.dt.bfloat16
U8 = mybir.dt.uint8
I32 = mybir.dt.int32
FP4X4 = mybir.dt.float4_e2m1fn_x4
ADD = mybir.AluOpType.add
SUB = mybir.AluOpType.subtract
MULT = mybir.AluOpType.mult
SIGMOID = mybir.ActivationFunctionType.Sigmoid
TANH = mybir.ActivationFunctionType.Tanh

B, IN, L = 512, 1024, 1536
FLOPS = 2 * B * IN * 3 * L

P = 128
G = IN // 512
T = B // P
UNITS = L // P
BLOCKS = ((0, 512), (512, 1536))


def tile_grucellstack_pa_kernel(
    tc, input_words, input_scales, h0, gh0, W_ih0_words, W_ih0_scales, b_ih0, out
):
    nc = tc.nc
    with ExitStack() as ctx:
        keep = ctx.enter_context(tc.tile_pool(name="keep", bufs=1))
        work = ctx.enter_context(tc.tile_pool(name="work", bufs=3))
        ps_mx = ctx.enter_context(tc.psum_pool(name="ps_mx", bufs=4))
        ps_gh = ctx.enter_context(tc.psum_pool(name="ps_gh", bufs=2))
        ps_n = ctx.enter_context(tc.psum_pool(name="ps_n", bufs=2))
        ctx.enter_context(tc.manual_schedule())

        gh_v = gh0.rearrange("(t p) c -> p t c", p=P)
        h_v = h0.rearrange("(t p) c -> p t c", p=P)
        out_v = out.rearrange("(t p) c -> p t c", p=P)
        w_v = W_ih0_words.rearrange("g p c -> p g c")

        x = keep.tile([P, G, 2 * B], U8, align_bytes=64)
        xs = keep.tile([P, G, B], U8, align_bytes=64)
        ws_r = keep.tile([P, G, L], U8, align_bytes=64)
        ws_zn = keep.tile([P, G, 2 * L], U8, align_bytes=64)
        brow = keep.tile([P, P], BF16)
        warm = keep.tile([P, 1], F32)
        bcol = keep.tile([P, 3 * UNITS], F32)
        bcol_h = keep.tile([P, 3 * UNITS], BF16)
        bz = keep.tile([P, L], BF16)
        id_h = keep.tile([P, P], BF16)
        id_f = keep.tile([P, P], F32)
        w, gh, h = {}, {}, {}
        for k, (c0, c1) in enumerate(BLOCKS):
            for q in "rzn":
                w[q, k] = keep.tile([P, G, 2 * (c1 - c0)], U8, align_bytes=64, name="w_%s%d" % (q, k))
                gh[q, k] = keep.tile([P, T, c1 - c0], BF16, name="gh_%s%d" % (q, k))
            h[k] = keep.tile([P, T, c1 - c0], BF16, name="h_%d" % k)
        base = {"r": 0, "z": L, "n": 2 * L}

        def load_w(q, k):
            c0, c1 = BLOCKS[k]
            nc.sync.dma_start(
                out=w[q, k][:].bitcast(I32),
                in_=w_v[:, :, 2 * (base[q] + c0) : 2 * (base[q] + c1)].bitcast(I32),
            )

        def load_gh(eng, q, k):
            c0, c1 = BLOCKS[k]
            eng.dma_start(out=gh[q, k][:], in_=gh_v[:, :, base[q] + c0 : base[q] + c1])

        def load_h(k):
            c0, c1 = BLOCKS[k]
            nc.sync.dma_start(out=h[k][:], in_=h_v[:, :, c0:c1])

        def load_scales(tile, src):
            for q in range(4):
                nc.sync.dma_start(
                    out=tile[32 * q : 32 * q + 4, :, :].bitcast(I32),
                    in_=src[:, 4 * q : 4 * q + 4, :].rearrange("g r n -> r g n").bitcast(I32),
                )

        load_gh(nc.gpsimd, "r", 0)
        load_gh(nc.gpsimd, "n", 0)
        make_identity(nc, id_h[:])
        make_identity(nc, id_f[:])
        nc.vector.memset(xs[:].bitcast(I32), 0)
        nc.vector.memset(ws_r[:].bitcast(I32), 0)
        nc.vector.memset(brow[:], 0.0)
        nc.vector.memset(warm[:], 0.0)
        nc.vector.memset(ws_zn[:].bitcast(I32), 0)
        nc.scalar.activation(out=warm[:], in_=warm[:], func=SIGMOID)
        load_w("r", 0)
        nc.sync.dma_start(out=x[:].bitcast(I32), in_=input_words.rearrange("g p c -> p g c").bitcast(I32))
        load_scales(xs, input_scales)
        load_scales(ws_r, W_ih0_scales[:, :, 0:L])
        nc.sync.dma_start(out=brow[0 : 3 * UNITS, :], in_=b_ih0.rearrange("(r c) -> r c", c=P))
        load_w("z", 0)
        load_gh(nc.sync, "z", 0)
        load_scales(ws_zn, W_ih0_scales[:, :, L : 3 * L])
        load_w("n", 0)
        load_h(0)
        for q in "rzn":
            load_w(q, 1)
            if q == "r":
                load_gh(nc.sync, "r", 1)
                load_gh(nc.sync, "n", 1)
            if q == "z":
                load_gh(nc.sync, "z", 1)
        load_h(1)

        t16 = ps_gh.tile([P, 2, B], BF16, name="t16")
        nc.tensor.transpose(t16[:, 0, 0:P], brow[:], id_h[:])
        nc.vector.tensor_copy(out=bcol_h[:], in_=t16[:, 0, 0 : 3 * UNITS])
        nc.vector.tensor_copy(out=bcol[:], in_=t16[:, 0, 0 : 3 * UNITS])
        for half in range(2):
            cols = 1024 if half == 0 else 512
            t16 = ps_gh.tile([P, 2, B], BF16, name="t16")
            flat = t16[:].rearrange("p a b -> p (a b)")
            for j in range(cols // P):
                u = 8 * half + j
                nc.tensor.transpose(
                    flat[:, P * j : P * (j + 1)],
                    bcol_h[:, UNITS + u : UNITS + u + 1].to_broadcast([P, P]),
                    id_h[:],
                )
            nc.scalar.copy(out=bz[:, 1024 * half : 1024 * half + cols], in_=flat[:, 0:cols])

        ps_r, ps_z, ps_nn, ght_ps, ghrt, ghzb = {}, {}, {}, {}, {}, {}
        r_t, m2_t, n_t, ntok, z_t, d_t, e_t, o_t = {}, {}, {}, {}, {}, {}, {}, {}

        def loc(u):
            k = 0 if u < 4 else 1
            return k, P * u - BLOCKS[k][0]

        def ghzb_add(u):
            k, c = loc(u)
            g = work.tile([P, T, P], F32, name="ghzb")
            nc.gpsimd.tensor_tensor(
                out=g[:],
                in0=gh["z", k][:, :, c : c + P],
                in1=bz[:, P * u : P * (u + 1)].unsqueeze(1).to_broadcast([P, T, P]),
                op=ADD,
            )
            ghzb[u] = g

        def gh_transpose(u):
            k, c = loc(u)
            t = ps_gh.tile([P, 2, B], BF16, name="t16")
            for i, q in enumerate("rn"):
                for j in range(T):
                    nc.tensor.transpose(t[:, i, P * j : P * (j + 1)], gh[q, k][:, j, c : c + P], id_h[:])
            ght_ps[u] = t

        def gh_copy(u):
            s = work.tile([P, B], BF16, name="ghr_t")
            nc.scalar.copy(out=s[:], in_=ght_ps[u][:, 0, :])
            ghrt[u] = s

        def mx(u):
            k, c = loc(u)
            col = P * u

            def weights_stationary(q, plane, off):
                acc = ps_mx.tile([P, B], F32, name="acc")
                for g in range(G):
                    nc.tensor.matmul_mx(
                        out=acc[:],
                        lhsT=w[q, k][:, g, 2 * c : 2 * (c + P)].bitcast(FP4X4),
                        lhsT_scale=plane[:, g, off + col : off + col + P],
                        rhs=x[:, g, :].bitcast(FP4X4),
                        rhs_scale=xs[:, g, :],
                        start=(g == 0),
                        stop=(g == G - 1),
                    )
                return acc

            ps_r[u] = weights_stationary("r", ws_r, 0)
            accz = ps_mx.tile([P, B], F32, name="acc")
            for j in range(T):
                for g in range(G):
                    nc.tensor.matmul_mx(
                        out=accz[:, P * j : P * (j + 1)],
                        lhsT=x[:, g, 2 * P * j : 2 * P * (j + 1)].bitcast(FP4X4),
                        lhsT_scale=xs[:, g, P * j : P * (j + 1)],
                        rhs=w["z", k][:, g, 2 * c : 2 * (c + P)].bitcast(FP4X4),
                        rhs_scale=ws_zn[:, g, col : col + P],
                        start=(g == 0),
                        stop=(g == G - 1),
                    )
            ps_z[u] = accz
            ps_nn[u] = weights_stationary("n", ws_zn, L)

        def tok(ap):
            return ap.rearrange("p (t c) -> p t c", t=T)

        for i in range(-1, UNITS + 2):
            if 0 <= i - 1 < UNITS:
                u = i - 1
                n_c = work.tile([P, B], F32, name="n_c")
                nc.scalar.activation(
                    out=n_c[:], in_=m2_t[u][:], func=TANH, bias=bcol[:, 2 * UNITS + u : 2 * UNITS + u + 1]
                )
                n_t[u] = n_c
            if i + 1 < UNITS:
                gh_transpose(i + 1)
            if 0 <= i - 1 < UNITS:
                u = i - 1
                nt = ps_n.tile([P, B], F32, name="nt")
                for j in range(T):
                    nc.tensor.transpose(nt[:, P * j : P * (j + 1)], n_t[u][:, P * j : P * (j + 1)], id_f[:])
                ntok[u] = nt
            if i + 1 < UNITS:
                mx(i + 1)
            if i == -1:
                gh_copy(0)
                ghzb_add(0)
                ghzb_add(1)
                continue
            if i < UNITS:
                a = work.tile([P, B], F32, name="a")
                nc.vector.tensor_tensor(out=a[:], in0=ps_r[i][:], in1=ghrt[i][:], op=ADD)
                r = work.tile([P, B], F32, name="r")
                nc.scalar.activation(out=r[:], in_=a[:], func=SIGMOID, bias=bcol[:, i : i + 1])
                r_t[i] = r
                cz = work.tile([P, B], F32, name="cz")
                nc.vector.tensor_tensor(
                    out=cz[:], in0=ps_z[i][:], in1=ghzb[i][:].rearrange("p t c -> p (t c)"), op=ADD
                )
                z = work.tile([P, B], F32, name="z")
                nc.scalar.activation(out=z[:], in_=cz[:], func=SIGMOID)
                z_t[i] = z
            if i + 1 < UNITS:
                gh_copy(i + 1)
            if 0 <= i - 2:
                u = i - 2
                if u < UNITS - 2:
                    if u % 2 == 0:
                        o2 = work.tile([P, T, 2 * P], F32, name="o2")
                        o_t[u], o_t[u + 1] = o2, o2
                    dst = o_t[u][:, :, P * (u % 2) : P * (u % 2 + 1)]
                else:
                    o1 = work.tile([P, T, P], F32, name="o1")
                    dst = o1[:]
                nc.vector.tensor_tensor(out=dst, in0=tok(ntok[u][:]), in1=tok(e_t[u][:]), op=ADD)
                if u >= UNITS - 2:
                    nc.sync.dma_start(out=out_v[:, :, P * u : P * (u + 1)], in_=dst)
                elif u % 2 == 1:
                    nc.sync.dma_start(out=out_v[:, :, P * (u - 1) : P * (u + 1)], in_=o_t[u][:])
            if i < UNITS:
                m = work.tile([P, B], F32, name="m")
                nc.vector.tensor_tensor(out=m[:], in0=r_t[i][:], in1=ght_ps[i][:, 1, :], op=MULT)
            if 0 <= i - 1 < UNITS:
                u = i - 1
                k, c = loc(u)
                d = work.tile([P, B], F32, name="d")
                nc.vector.tensor_tensor(out=tok(d[:]), in0=h[k][:, :, c : c + P], in1=tok(ntok[u][:]), op=SUB)
                e = work.tile([P, B], F32, name="e")
                nc.gpsimd.tensor_tensor(out=e[:], in0=z_t[u][:], in1=d[:], op=MULT)
                e_t[u] = e
            if i + 2 < UNITS:
                ghzb_add(i + 2)
            if i < UNITS:
                m2 = work.tile([P, B], F32, name="m2")
                nc.vector.tensor_tensor(out=m2[:], in0=ps_nn[i][:], in1=m[:], op=ADD)
                m2_t[i] = m2
